import numpy as np
import ml_dtypes


def mxq(x, axis, fmt="e4m3"):
    dtype, down = {"e4m3": (ml_dtypes.float8_e4m3fn, 7), "e5m2": (ml_dtypes.float8_e5m2, 14)}[fmt]
    v = np.moveaxis(np.asarray(x, np.float32).astype(ml_dtypes.bfloat16).astype(np.float64), axis, -1)
    blocks = v.reshape(v.shape[:-1] + (-1, 32))
    amax = np.abs(blocks).max(-1, keepdims=True)
    byte = np.maximum(np.where(amax > 0, np.frexp(amax)[1] - 1 + 127, 0) - down, 1)
    scale = np.exp2(byte - 127.0)
    codes = (blocks / scale).astype(np.float32).astype(dtype).astype(np.float64)
    return np.moveaxis((codes * scale).reshape(v.shape), -1, axis)


WIDE = False


def mx_kscale(k):
    if not WIDE:
        return np.ones(k)
    levels = np.array([10, -10, 5, -5, 0])
    a = np.random.permutation(np.resize(levels, k // 512 * 4)).reshape(k // 512, 4)
    idx = np.arange(k)
    return np.exp2(a[idx // 512, idx % 128 // 32])


BF16 = ml_dtypes.bfloat16


def bf(x):
    return np.asarray(x, np.float32).astype(BF16)


def f64(x):
    return np.asarray(x).astype(np.float64)


E2M1 = np.array([0.0, 0.5, 1.0, 1.5, 2.0, 3.0, 4.0, 6.0, -0.0, -0.5, -1.0, -1.5, -2.0, -3.0, -4.0, -6.0])


def pack_weight(w, fmt):
    k, n = w.shape
    w = f64(bf(w)).reshape(k // 32, 32, n)
    amax = np.abs(w).max(1)
    if fmt == "e4m3":
        byte = np.frexp(amax)[1] - 1 + 127 - 7
    else:
        mant, ex = np.frexp(amax / 6.0)
        byte = np.where(mant > 0.5, ex, ex - 1) + 127
    byte = np.clip(np.where(amax > 0, byte, 1), 1, 254)
    scaled = (w * np.exp2(127.0 - byte)[:, None, :]).reshape(k, n).astype(np.float32)
    by_word = np.ascontiguousarray(scaled.reshape(k // 512, 128, 4, n).transpose(0, 1, 3, 2))
    if fmt == "e4m3":
        words = by_word.astype(ml_dtypes.float8_e4m3fn).view(np.uint8)
    else:
        c = by_word.astype(ml_dtypes.float4_e2m1fn).view(np.uint8) & 0xF
        words = c[..., 0::2] | (c[..., 1::2] << 4)
    return np.ascontiguousarray(words), np.ascontiguousarray(byte.astype(np.uint8).reshape(k // 512, 16, n))


def unpack_weight(words, scales, fmt):
    g, p, n, _ = words.shape
    if fmt == "e4m3":
        vals = np.ascontiguousarray(words).view(ml_dtypes.float8_e4m3fn).astype(np.float64)
    else:
        nib = np.empty((g, p, n, 4), np.uint8)
        nib[..., 0::2] = words & 0xF
        nib[..., 1::2] = words >> 4
        vals = E2M1[nib]
    vals = vals * np.repeat(np.exp2(scales.astype(np.float64) - 127.0), 8, axis=1)[..., None]
    return vals.transpose(0, 1, 3, 2).reshape(g * 512, n)


B, I, H = 128, 1024, 2048
MXK = 16 * 32
FMT = "e4m3"


def sigmoid(v):
    return 1.0 / (1.0 + np.exp(-v))


def lin(a, wt):
    if a.shape[1] % MXK == 0:
        return mxq(a, 1, "e4m3") @ wt
    return a @ wt


def setup_inputs():
    s = mx_kscale(I)
    t = mx_kscale(H) if H % MXK == 0 else np.ones(H)
    inp = {"incoming": bf(np.random.standard_normal((B, I)) * s),
           "old_h": bf(np.random.standard_normal((B, H)) * t),
           "old_c": bf(np.random.standard_normal((B, H)))}
    for n in ("i", "o", "f", "c"):
        words, scales = pack_weight((np.random.standard_normal((H, I)) / np.sqrt(I) / s).T, FMT)
        inp["w_" + n + "_words"] = words
        inp["w_" + n + "_scales"] = scales
        inp["b_" + n] = bf(np.random.standard_normal(H) * 0.5)
        words, scales = pack_weight((np.random.standard_normal((H, H)) / np.sqrt(H) / t).T, FMT)
        inp["u_" + n + "_words"] = words
        inp["u_" + n + "_scales"] = scales
    return inp


def reference(incoming, old_h, old_c, w_i_words, w_i_scales, b_i, u_i_words, u_i_scales, w_o_words, w_o_scales, b_o, u_o_words, u_o_scales, w_f_words, w_f_scales, b_f, u_f_words, u_f_scales, w_c_words, w_c_scales, b_c, u_c_words, u_c_scales):
    W = np.concatenate([unpack_weight(w_i_words, w_i_scales, FMT), unpack_weight(w_o_words, w_o_scales, FMT),
                        unpack_weight(w_f_words, w_f_scales, FMT), unpack_weight(w_c_words, w_c_scales, FMT)], axis=1)
    U = np.concatenate([unpack_weight(u_i_words, u_i_scales, FMT), unpack_weight(u_o_words, u_o_scales, FMT),
                        unpack_weight(u_f_words, u_f_scales, FMT), unpack_weight(u_c_words, u_c_scales, FMT)], axis=1)
    b = np.concatenate([f64(b_i), f64(b_o), f64(b_f), f64(b_c)], axis=0)
    gates = lin(f64(incoming), W) + lin(f64(old_h), U) + b
    gi, go, gf, gc = np.split(gates, 4, axis=-1)
    i = sigmoid(gi)
    o = sigmoid(go)
    f = sigmoid(gf)
    c_tilde = np.tanh(gc)
    new_c = f * f64(old_c) + i * c_tilde
    new_h = o * np.tanh(new_c)
    return (new_h, new_c)

@@ -1,0 +1,207 @@
+from contextlib import ExitStack
+
+import concourse.mybir as mybir
+from concourse.masks import make_identity
+
+F32 = mybir.dt.float32
+BF16 = mybir.dt.bfloat16
+I32 = mybir.dt.int32
+U32 = mybir.dt.uint32
+U8 = mybir.dt.uint8
+FP8X4 = mybir.dt.float8_e4m3fn_x4
+ACT = mybir.ActivationFunctionType
+
+P = 128
+IN_FEATURES = 1024
+HIDDEN = 2048
+PACK = 4
+K_PASS = P * PACK
+W_PASSES = IN_FEATURES // K_PASS
+U_PASSES = HIDDEN // K_PASS
+PASSES = W_PASSES + U_PASSES
+BANK = 512
+BLOCKS = HIDDEN // BANK
+QUADRANTS = 4
+LIVE_ROWS = 4
+WORDS_PER_PASS = K_PASS // 2
+
+GATE_ORDER = ("i", "c", "f", "o")
+WEIGHT_BUFFERS = 8
+
+FLOPS = 2 * P * (IN_FEATURES + HIDDEN) * 4 * HIDDEN
+
+
+def block_columns(j):
+    return slice(j * BANK, (j + 1) * BANK)
+
+
+def tile_lstmcell_w_kernel(
+    tc,
+    incoming, old_h, old_c,
+    w_i_words, w_i_scales, b_i, u_i_words, u_i_scales,
+    w_o_words, w_o_scales, b_o, u_o_words, u_o_scales,
+    w_f_words, w_f_scales, b_f, u_f_words, u_f_scales,
+    w_c_words, w_c_scales, b_c, u_c_words, u_c_scales,
+    out_0, out_1,
+):
+    nc = tc.nc
+    new_h_out, new_c_out = out_0, out_1
+    w_words = {"i": w_i_words, "o": w_o_words, "f": w_f_words, "c": w_c_words}
+    w_scales = {"i": w_i_scales, "o": w_o_scales, "f": w_f_scales, "c": w_c_scales}
+    u_words = {"i": u_i_words, "o": u_o_words, "f": u_f_words, "c": u_c_words}
+    u_scales = {"i": u_i_scales, "o": u_o_scales, "f": u_f_scales, "c": u_c_scales}
+    bias = {"i": b_i, "o": b_o, "f": b_f, "c": b_c}
+
+    with ExitStack() as ctx:
+        keep = ctx.enter_context(tc.tile_pool(name="keep", bufs=1))
+        stream = ctx.enter_context(tc.tile_pool(name="stream", bufs=WEIGHT_BUFFERS))
+        work = ctx.enter_context(tc.tile_pool(name="work", bufs=4))
+        psum = ctx.enter_context(tc.psum_pool(name="psum", bufs=8))
+
+        table_warm = keep.tile([P, 1], F32)
+        nc.vector.memset(table_warm[:], 0.0)
+        nc.scalar.activation(out=table_warm[:], in_=table_warm[:], func=ACT.Sigmoid)
+
+        identity_f32 = keep.tile([P, P], F32)
+        make_identity(nc, identity_f32[:])
+        identity_bf16 = keep.tile([P, P], BF16)
+        make_identity(nc, identity_bf16[:])
+
+        x_rows = keep.tile([P, IN_FEATURES + HIDDEN], BF16)
+        nc.sync.dma_start(out=x_rows[:, :IN_FEATURES], in_=incoming)
+        nc.sync.dma_start(out=x_rows[:, IN_FEATURES:], in_=old_h)
+
+        bias_rows = keep.tile([P, HIDDEN], BF16)
+        nc.vector.memset(bias_rows[:], 0.0)
+        for n, gate in enumerate(GATE_ORDER):
+            nc.scalar.dma_start(out=bias_rows[n : n + 1, :], in_=bias[gate].unsqueeze(0))
+
+        sheets = keep.tile([P, 4 + 2, HIDDEN], U8, align_bytes=64)
+        for s in range(4 + 2):
+            nc.vector.memset(sheets[:, s, :].bitcast(I32), 0)
+
+        def plane_place(n, c):
+            if c < W_PASSES:
+                return 4 + n // 2, LIVE_ROWS * (W_PASSES * (n % 2) + c)
+            return n, LIVE_ROWS * (c - W_PASSES)
+
+        for n, gate in enumerate(GATE_ORDER):
+            w_sheet, w_first = plane_place(n, 0)
+            u_sheet, u_first = plane_place(n, W_PASSES)
+            for quadrant in range(QUADRANTS):
+                rows = slice(LIVE_ROWS * quadrant, LIVE_ROWS * (quadrant + 1))
+                w_start = 32 * quadrant + w_first
+                nc.sync.dma_start(
+                    out=sheets[w_start : w_start + W_PASSES * LIVE_ROWS, w_sheet, :].bitcast(I32),
+                    in_=w_scales[gate][:, rows, :].bitcast(I32),
+                )
+                u_start = 32 * quadrant + u_first
+                nc.sync.dma_start(
+                    out=sheets[u_start : u_start + U_PASSES * LIVE_ROWS, u_sheet, :].bitcast(I32),
+                    in_=u_scales[gate][:, rows, :].bitcast(I32),
+                )
+
+        x_words = x_rows[:].bitcast(F32)
+        grouped = keep.tile([P, PASSES, P, PACK], BF16, align_bytes=64)
+        for pair in range(PASSES // 2):
+            flipped = psum.tile([P, 2, 2, P], F32, tag="bank")
+            for s in range(2):
+                first_word = (2 * pair + s) * WORDS_PER_PASS
+                for half in range(2):
+                    nc.tensor.transpose(
+                        flipped[:, s, half, :],
+                        x_words[:, first_word + half : first_word + WORDS_PER_PASS : 2],
+                        identity_f32[:],
+                    )
+            nc.vector.tensor_copy(
+                out=grouped[:, 2 * pair : 2 * pair + 2, :, :].bitcast(F32),
+                in_=flipped[:].rearrange("p s half b -> p s b half"),
+            )
+        x_codes = keep.tile([P, PASSES * P], U32, align_bytes=64)
+        x_scales = keep.tile([P, PASSES * P], U8, align_bytes=64)
+        for pair in range(PASSES // 2):
+            columns = slice(2 * pair * P, (2 * pair + 2) * P)
+            nc.vector.quantize_mx(
+                out=x_codes[:, columns].bitcast(FP8X4),
+                scales=x_scales[:, columns],
+                in_=grouped[:, 2 * pair : 2 * pair + 2, :, :].rearrange("p s b t -> p (s b t)"),
+            )
+
+        bias_all_rows = keep.tile([P, 4, HIDDEN], F32)
+        for n in range(4):
+            for j in range(BLOCKS):
+                spread = psum.tile([P, BANK], F32, tag="bank")
+                nc.tensor.matmul(
+                    spread[:],
+                    lhsT=identity_bf16[:, n : n + 1].to_broadcast([P, P]),
+                    rhs=bias_rows[:, block_columns(j)],
+                    start=True,
+                    stop=True,
+                )
+                if j % 2 == 0:
+                    nc.scalar.copy(out=bias_all_rows[:, n, block_columns(j)], in_=spread[:])
+                else:
+                    nc.vector.tensor_copy(out=bias_all_rows[:, n, block_columns(j)], in_=spread[:])
+
+        old_c_rows = keep.tile([P, HIDDEN], BF16)
+        gate_value = {}
+        input_term = keep.tile([P, HIDDEN], F32)
+        new_c = keep.tile([P, HIDDEN], F32)
+        tanh_new_c = keep.tile([P, HIDDEN], F32)
+
+        for n, gate in enumerate(GATE_ORDER):
+            if gate == "f":
+                nc.sync.dma_start(out=old_c_rows[:], in_=old_c)
+
+            sums = [
+                psum.tile([P, BANK], F32, tag="bank", name="sums_%s_%d" % (gate, j))
+                for j in range(BLOCKS)
+            ]
+            for c in range(PASSES):
+                source = w_words[gate][c] if c < W_PASSES else u_words[gate][c - W_PASSES]
+                codes = stream.tile([P, HIDDEN], U32, align_bytes=64)
+                nc.sync.dma_start(
+                    out=codes[:].bitcast(I32),
+                    in_=source.rearrange("p n t -> p (n t)").bitcast(I32),
+                )
+                sheet, first = plane_place(n, c)
+                for j in range(BLOCKS):
+                    nc.tensor.matmul_mx(
+                        out=sums[j][:],
+                        lhsT=x_codes[:, c * P : (c + 1) * P].bitcast(FP8X4),
+                        lhsT_scale=x_scales[:, c * P : (c + 1) * P],
+                        rhs=codes[:, block_columns(j)].bitcast(FP8X4),
+                        rhs_scale=sheets[first:P, sheet, block_columns(j)],
+                        start=(c == 0),
+                        stop=(c == PASSES - 1),
+                    )
+
+            gate_value[gate] = keep.tile([P, HIDDEN], F32, name="gate_" + gate)
+            for j in range(BLOCKS):
+                with_bias = work.tile([P, BANK], F32)
+                nc.vector.tensor_add(
+                    out=with_bias[:], in0=sums[j][:], in1=bias_all_rows[:, n, block_columns(j)]
+                )
+                nc.scalar.activation(
+                    out=gate_value[gate][:, block_columns(j)],
+                    in_=with_bias[:],
+                    func=ACT.Tanh if gate == "c" else ACT.Sigmoid,
+                )
+
+            for j in range(BLOCKS):
+                cols = block_columns(j)
+                if gate == "c":
+                    nc.vector.tensor_mul(
+                        out=input_term[:, cols], in0=gate_value["i"][:, cols], in1=gate_value["c"][:, cols]
+                    )
+                if gate == "f":
+                    kept = work.tile([P, BANK], F32)
+                    nc.vector.tensor_mul(out=kept[:], in0=gate_value["f"][:, cols], in1=old_c_rows[:, cols])
+                    nc.vector.tensor_add(out=new_c[:, cols], in0=kept[:], in1=input_term[:, cols])
+                    nc.scalar.activation(out=tanh_new_c[:, cols], in_=new_c[:, cols], func=ACT.Tanh)
+                if gate == "o":
+                    new_h = work.tile([P, BANK], F32)
+                    nc.vector.tensor_mul(out=new_h[:], in0=gate_value["o"][:, cols], in1=tanh_new_c[:, cols])
+                    nc.sync.dma_start(out=new_h_out[:, cols], in_=new_h[:])
+            if gate == "f":
+                nc.scalar.dma_start(out=new_c_out, in_=new_c[:])

@@ -91,14 +91,14 @@ def tile_lstmcell_w_kernel(
             for quadrant in range(QUADRANTS):
                 rows = slice(LIVE_ROWS * quadrant, LIVE_ROWS * (quadrant + 1))
                 w_start = 32 * quadrant + w_first
-                nc.sync.dma_start(
-                    out=sheets[w_start : w_start + W_PASSES * LIVE_ROWS, w_sheet, :].bitcast(I32),
-                    in_=w_scales[gate][:, rows, :].bitcast(I32),
+                nc.gpsimd.dma_start(
+                    out=sheets[w_start : w_start + W_PASSES * LIVE_ROWS, w_sheet, :].bitcast(F32),
+                    in_=w_scales[gate][:, rows, :].bitcast(F32),
                 )
                 u_start = 32 * quadrant + u_first
-                nc.sync.dma_start(
-                    out=sheets[u_start : u_start + U_PASSES * LIVE_ROWS, u_sheet, :].bitcast(I32),
-                    in_=u_scales[gate][:, rows, :].bitcast(I32),
+                nc.gpsimd.dma_start(
+                    out=sheets[u_start : u_start + U_PASSES * LIVE_ROWS, u_sheet, :].bitcast(F32),
+                    in_=u_scales[gate][:, rows, :].bitcast(F32),
                 )
 
         x_words = x_rows[:].bitcast(F32)

@@ -57,6 +57,7 @@ def tile_lstmcell_w_kernel(
         stream = ctx.enter_context(tc.tile_pool(name="stream", bufs=WEIGHT_BUFFERS))
         work = ctx.enter_context(tc.tile_pool(name="work", bufs=4))
         psum = ctx.enter_context(tc.psum_pool(name="psum", bufs=8))
+        ctx.enter_context(tc.manual_schedule(engines={mybir.EngineType.SP}))
 
         table_warm = keep.tile([P, 1], F32)
         nc.vector.memset(table_warm[:], 0.0)
@@ -149,7 +150,18 @@ def tile_lstmcell_w_kernel(
         new_c = keep.tile([P, HIDDEN], F32)
         tanh_new_c = keep.tile([P, HIDDEN], F32)
 
-        for n, gate in enumerate(GATE_ORDER):
+        def gate_block(n, gate, j, sums_j, out_tile):
+            with_bias = work.tile([P, BANK], F32, name="with_bias")
+            nc.vector.tensor_add(
+                out=with_bias[:], in0=sums_j[:], in1=bias_all_rows[:, n, block_columns(j)]
+            )
+            nc.scalar.activation(
+                out=out_tile[:, block_columns(j)],
+                in_=with_bias[:],
+                func=ACT.Tanh if gate == "c" else ACT.Sigmoid,
+            )
+
+        for n, gate in enumerate(GATE_ORDER[:3]):
             if gate == "f":
                 nc.sync.dma_start(out=old_c_rows[:], in_=old_c)
 
@@ -159,7 +171,7 @@ def tile_lstmcell_w_kernel(
             ]
             for c in range(PASSES):
                 source = w_words[gate][c] if c < W_PASSES else u_words[gate][c - W_PASSES]
-                codes = stream.tile([P, HIDDEN], U32, align_bytes=64)
+                codes = stream.tile([P, HIDDEN], U32, align_bytes=64, tag="codes", name="codes")
                 nc.sync.dma_start(
                     out=codes[:].bitcast(I32),
                     in_=source.rearrange("p n t -> p (n t)").bitcast(I32),
@@ -178,15 +190,7 @@ def tile_lstmcell_w_kernel(
 
             gate_value[gate] = keep.tile([P, HIDDEN], F32, name="gate_" + gate)
             for j in range(BLOCKS):
-                with_bias = work.tile([P, BANK], F32)
-                nc.vector.tensor_add(
-                    out=with_bias[:], in0=sums[j][:], in1=bias_all_rows[:, n, block_columns(j)]
-                )
-                nc.scalar.activation(
-                    out=gate_value[gate][:, block_columns(j)],
-                    in_=with_bias[:],
-                    func=ACT.Tanh if gate == "c" else ACT.Sigmoid,
-                )
+                gate_block(n, gate, j, sums[j], gate_value[gate])
 
             for j in range(BLOCKS):
                 cols = block_columns(j)
@@ -195,13 +199,57 @@ def tile_lstmcell_w_kernel(
                         out=input_term[:, cols], in0=gate_value["i"][:, cols], in1=gate_value["c"][:, cols]
                     )
                 if gate == "f":
-                    kept = work.tile([P, BANK], F32)
+                    kept = work.tile([P, BANK], F32, name="kept")
                     nc.vector.tensor_mul(out=kept[:], in0=gate_value["f"][:, cols], in1=old_c_rows[:, cols])
                     nc.vector.tensor_add(out=new_c[:, cols], in0=kept[:], in1=input_term[:, cols])
                     nc.scalar.activation(out=tanh_new_c[:, cols], in_=new_c[:, cols], func=ACT.Tanh)
-                if gate == "o":
-                    new_h = work.tile([P, BANK], F32)
-                    nc.vector.tensor_mul(out=new_h[:], in0=gate_value["o"][:, cols], in1=tanh_new_c[:, cols])
-                    nc.sync.dma_start(out=new_h_out[:, cols], in_=new_h[:])
-            if gate == "f":
-                nc.scalar.dma_start(out=new_c_out, in_=new_c[:])
+
+        n = 3
+        gate_value["o"] = keep.tile([P, HIDDEN], F32, name="gate_o")
+        new_h = keep.tile([P, HIDDEN], F32)
+        w_by_block = w_words["o"].rearrange("g p n t -> p g (n t)")
+        u_by_block = u_words["o"].rearrange("g p n t -> p g (n t)")
+        for j in range(BLOCKS):
+            cols = block_columns(j)
+            code_bytes = slice(j * BANK * PACK, (j + 1) * BANK * PACK)
+            u_codes = stream.tile([P, HIDDEN], U32, align_bytes=64, tag="codes", name="u_codes")
+            nc.sync.dma_start(
+                out=u_codes[:].rearrange("p (g n) -> p g n", g=U_PASSES).bitcast(I32),
+                in_=u_by_block[:, :, code_bytes].bitcast(I32),
+            )
+            w_codes = stream.tile([P, HIDDEN], U32, align_bytes=64, tag="codes", name="w_codes")
+            if j < BLOCKS - 1:
+                nc.sync.dma_start(
+                    out=w_codes[:, : W_PASSES * BANK].rearrange("p (g n) -> p g n", g=W_PASSES).bitcast(I32),
+                    in_=w_by_block[:, :, code_bytes].bitcast(I32),
+                )
+            else:
+                for g in range(W_PASSES):
+                    nc.sync.dma_start(
+                        out=w_codes[:, g * BANK : (g + 1) * BANK].bitcast(I32),
+                        in_=w_by_block[:, g, code_bytes].bitcast(I32),
+                    )
+            sums_j = psum.tile([P, BANK], F32, tag="bank", name="sums_o_%d" % j)
+            order = list(range(W_PASSES, PASSES)) + list(range(W_PASSES))
+            for position, c in enumerate(order):
+                if c < W_PASSES:
+                    rhs = w_codes[:, c * BANK : (c + 1) * BANK]
+                else:
+                    rhs = u_codes[:, (c - W_PASSES) * BANK : (c - W_PASSES + 1) * BANK]
+                sheet, first = plane_place(n, c)
+                nc.tensor.matmul_mx(
+                    out=sums_j[:],
+                    lhsT=x_codes[:, c * P : (c + 1) * P].bitcast(FP8X4),
+                    lhsT_scale=x_scales[:, c * P : (c + 1) * P],
+                    rhs=rhs.bitcast(FP8X4),
+                    rhs_scale=sheets[first:P, sheet, cols],
+                    start=(position == 0),
+                    stop=(position == PASSES - 1),
+                )
+            gate_block(n, "o", j, sums_j, gate_value["o"])
+            nc.vector.tensor_mul(out=new_h[:, cols], in0=gate_value["o"][:, cols], in1=tanh_new_c[:, cols])
+
+        done = (BLOCKS - 1) * BANK
+        nc.sync.dma_start(out=new_c_out, in_=new_c[:])
+        nc.sync.dma_start(out=new_h_out[:, :done], in_=new_h[:, :done])
+        nc.sync.dma_start(out=new_h_out[:, done:], in_=new_h[:, done:])

@@ -26,6 +26,7 @@ LIVE_ROWS = 4
 WORDS_PER_PASS = K_PASS // 2
 
 GATE_ORDER = ("i", "c", "f", "o")
+LOAD_PASSES = 2
 WEIGHT_BUFFERS = 8
 
 FLOPS = 2 * P * (IN_FEATURES + HIDDEN) * 4 * HIDDEN
@@ -128,7 +129,7 @@ def tile_lstmcell_w_kernel(
                 in_=grouped[:, 2 * pair : 2 * pair + 2, :, :].rearrange("p s b t -> p (s b t)"),
             )
 
-        bias_all_rows = keep.tile([P, 4, HIDDEN], F32)
+        bias_all_rows = keep.tile([P, 4, HIDDEN], BF16)
         for n in range(4):
             for j in range(BLOCKS):
                 spread = psum.tile([P, BANK], F32, tag="bank")
@@ -145,21 +146,30 @@ def tile_lstmcell_w_kernel(
                     nc.vector.tensor_copy(out=bias_all_rows[:, n, block_columns(j)], in_=spread[:])
 
         old_c_rows = keep.tile([P, HIDDEN], BF16)
-        gate_value = {}
-        input_term = keep.tile([P, HIDDEN], F32)
         new_c = keep.tile([P, HIDDEN], F32)
         tanh_new_c = keep.tile([P, HIDDEN], F32)
+        new_h = keep.tile([P, HIDDEN], F32)
 
-        def gate_block(n, gate, j, sums_j, out_tile):
+        def gate_block(n, gate, j, sums_j):
+            cols = block_columns(j)
             with_bias = work.tile([P, BANK], F32, name="with_bias")
-            nc.vector.tensor_add(
-                out=with_bias[:], in0=sums_j[:], in1=bias_all_rows[:, n, block_columns(j)]
-            )
+            nc.vector.tensor_add(out=with_bias[:], in0=sums_j[:], in1=bias_all_rows[:, n, cols])
+            if gate == "i":
+                nc.scalar.activation(out=new_c[:, cols], in_=with_bias[:], func=ACT.Sigmoid)
+                return
+            value = work.tile([P, BANK], F32, name="value")
             nc.scalar.activation(
-                out=out_tile[:, block_columns(j)],
-                in_=with_bias[:],
-                func=ACT.Tanh if gate == "c" else ACT.Sigmoid,
+                out=value[:], in_=with_bias[:], func=ACT.Tanh if gate == "c" else ACT.Sigmoid
             )
+            if gate == "c":
+                nc.vector.tensor_mul(out=new_c[:, cols], in0=new_c[:, cols], in1=value[:])
+            if gate == "f":
+                kept = work.tile([P, BANK], F32, name="kept")
+                nc.vector.tensor_mul(out=kept[:], in0=value[:], in1=old_c_rows[:, cols])
+                nc.vector.tensor_add(out=new_c[:, cols], in0=new_c[:, cols], in1=kept[:])
+                nc.scalar.activation(out=tanh_new_c[:, cols], in_=new_c[:, cols], func=ACT.Tanh)
+            if gate == "o":
+                nc.vector.tensor_mul(out=new_h[:, cols], in0=value[:], in1=tanh_new_c[:, cols])
 
         for n, gate in enumerate(GATE_ORDER[:3]):
             if gate == "f":
@@ -169,55 +179,44 @@ def tile_lstmcell_w_kernel(
                 psum.tile([P, BANK], F32, tag="bank", name="sums_%s_%d" % (gate, j))
                 for j in range(BLOCKS)
             ]
-            for c in range(PASSES):
-                source = w_words[gate][c] if c < W_PASSES else u_words[gate][c - W_PASSES]
-                codes = stream.tile([P, HIDDEN], U32, align_bytes=64, tag="codes", name="codes")
+            for first_pass in range(0, PASSES, LOAD_PASSES):
+                if first_pass < W_PASSES:
+                    source = w_words[gate][first_pass : first_pass + LOAD_PASSES]
+                else:
+                    source = u_words[gate][first_pass - W_PASSES : first_pass - W_PASSES + LOAD_PASSES]
+                codes = stream.tile([P, LOAD_PASSES * HIDDEN], U32, align_bytes=64, tag="codes", name="codes")
                 nc.sync.dma_start(
-                    out=codes[:].bitcast(I32),
-                    in_=source.rearrange("p n t -> p (n t)").bitcast(I32),
+                    out=codes[:].rearrange("p (g n) -> p g n", g=LOAD_PASSES).bitcast(I32),
+                    in_=source.rearrange("g p n t -> p g (n t)").bitcast(I32),
                 )
-                sheet, first = plane_place(n, c)
-                for j in range(BLOCKS):
-                    nc.tensor.matmul_mx(
-                        out=sums[j][:],
-                        lhsT=x_codes[:, c * P : (c + 1) * P].bitcast(FP8X4),
-                        lhsT_scale=x_scales[:, c * P : (c + 1) * P],
-                        rhs=codes[:, block_columns(j)].bitcast(FP8X4),
-                        rhs_scale=sheets[first:P, sheet, block_columns(j)],
-                        start=(c == 0),
-                        stop=(c == PASSES - 1),
-                    )
-
-            gate_value[gate] = keep.tile([P, HIDDEN], F32, name="gate_" + gate)
+                for c in range(first_pass, first_pass + LOAD_PASSES):
+                    sheet, first = plane_place(n, c)
+                    for j in range(BLOCKS):
+                        at = (c - first_pass) * HIDDEN + j * BANK
+                        nc.tensor.matmul_mx(
+                            out=sums[j][:],
+                            lhsT=x_codes[:, c * P : (c + 1) * P].bitcast(FP8X4),
+                            lhsT_scale=x_scales[:, c * P : (c + 1) * P],
+                            rhs=codes[:, at : at + BANK].bitcast(FP8X4),
+                            rhs_scale=sheets[first:P, sheet, block_columns(j)],
+                            start=(c == 0),
+                            stop=(c == PASSES - 1),
+                        )
             for j in range(BLOCKS):
-                gate_block(n, gate, j, sums[j], gate_value[gate])
-
-            for j in range(BLOCKS):
-                cols = block_columns(j)
-                if gate == "c":
-                    nc.vector.tensor_mul(
-                        out=input_term[:, cols], in0=gate_value["i"][:, cols], in1=gate_value["c"][:, cols]
-                    )
-                if gate == "f":
-                    kept = work.tile([P, BANK], F32, name="kept")
-                    nc.vector.tensor_mul(out=kept[:], in0=gate_value["f"][:, cols], in1=old_c_rows[:, cols])
-                    nc.vector.tensor_add(out=new_c[:, cols], in0=kept[:], in1=input_term[:, cols])
-                    nc.scalar.activation(out=tanh_new_c[:, cols], in_=new_c[:, cols], func=ACT.Tanh)
+                gate_block(n, gate, j, sums[j])
 
         n = 3
-        gate_value["o"] = keep.tile([P, HIDDEN], F32, name="gate_o")
-        new_h = keep.tile([P, HIDDEN], F32)
         w_by_block = w_words["o"].rearrange("g p n t -> p g (n t)")
         u_by_block = u_words["o"].rearrange("g p n t -> p g (n t)")
         for j in range(BLOCKS):
             cols = block_columns(j)
             code_bytes = slice(j * BANK * PACK, (j + 1) * BANK * PACK)
-            u_codes = stream.tile([P, HIDDEN], U32, align_bytes=64, tag="codes", name="u_codes")
+            u_codes = stream.tile([P, LOAD_PASSES * HIDDEN], U32, align_bytes=64, tag="codes", name="u_codes")
             nc.sync.dma_start(
-                out=u_codes[:].rearrange("p (g n) -> p g n", g=U_PASSES).bitcast(I32),
+                out=u_codes[:, : U_PASSES * BANK].rearrange("p (g n) -> p g n", g=U_PASSES).bitcast(I32),
                 in_=u_by_block[:, :, code_bytes].bitcast(I32),
             )
-            w_codes = stream.tile([P, HIDDEN], U32, align_bytes=64, tag="codes", name="w_codes")
+            w_codes = stream.tile([P, LOAD_PASSES * HIDDEN], U32, align_bytes=64, tag="codes", name="w_codes")
             if j < BLOCKS - 1:
                 nc.sync.dma_start(
                     out=w_codes[:, : W_PASSES * BANK].rearrange("p (g n) -> p g n", g=W_PASSES).bitcast(I32),
@@ -246,8 +245,7 @@ def tile_lstmcell_w_kernel(
                     start=(position == 0),
                     stop=(position == PASSES - 1),
                 )
-            gate_block(n, "o", j, sums_j, gate_value["o"])
-            nc.vector.tensor_mul(out=new_h[:, cols], in0=gate_value["o"][:, cols], in1=tanh_new_c[:, cols])
+            gate_block(n, "o", j, sums_j)
 
         done = (BLOCKS - 1) * BANK
         nc.sync.dma_start(out=new_c_out, in_=new_c[:])

@@ -150,104 +150,114 @@ def tile_lstmcell_w_kernel(
         tanh_new_c = keep.tile([P, HIDDEN], F32)
         new_h = keep.tile([P, HIDDEN], F32)
 
-        def gate_block(n, gate, j, sums_j):
-            cols = block_columns(j)
+        O_BLOCK_PASSES = 6
+        LAST_WIDTHS = (256, 256)
+
+        def gate_block(n, gate, cols, sums_g):
+            width = cols.stop - cols.start
             with_bias = work.tile([P, BANK], F32, name="with_bias")
-            nc.vector.tensor_add(out=with_bias[:], in0=sums_j[:], in1=bias_all_rows[:, n, cols])
+            nc.vector.tensor_add(out=with_bias[:, :width], in0=sums_g[:, :width], in1=bias_all_rows[:, n, cols])
             if gate == "i":
-                nc.scalar.activation(out=new_c[:, cols], in_=with_bias[:], func=ACT.Sigmoid)
+                nc.scalar.activation(out=new_c[:, cols], in_=with_bias[:, :width], func=ACT.Sigmoid)
                 return
             value = work.tile([P, BANK], F32, name="value")
             nc.scalar.activation(
-                out=value[:], in_=with_bias[:], func=ACT.Tanh if gate == "c" else ACT.Sigmoid
+                out=value[:, :width], in_=with_bias[:, :width], func=ACT.Tanh if gate == "c" else ACT.Sigmoid
             )
             if gate == "c":
-                nc.vector.tensor_mul(out=new_c[:, cols], in0=new_c[:, cols], in1=value[:])
+                nc.vector.tensor_mul(out=new_c[:, cols], in0=new_c[:, cols], in1=value[:, :width])
             if gate == "f":
                 kept = work.tile([P, BANK], F32, name="kept")
-                nc.vector.tensor_mul(out=kept[:], in0=value[:], in1=old_c_rows[:, cols])
-                nc.vector.tensor_add(out=new_c[:, cols], in0=new_c[:, cols], in1=kept[:])
+                nc.vector.tensor_mul(out=kept[:, :width], in0=value[:, :width], in1=old_c_rows[:, cols])
+                nc.vector.tensor_add(out=new_c[:, cols], in0=new_c[:, cols], in1=kept[:, :width])
                 nc.scalar.activation(out=tanh_new_c[:, cols], in_=new_c[:, cols], func=ACT.Tanh)
             if gate == "o":
-                nc.vector.tensor_mul(out=new_h[:, cols], in0=value[:], in1=tanh_new_c[:, cols])
+                nc.vector.tensor_mul(out=new_h[:, cols], in0=value[:, :width], in1=tanh_new_c[:, cols])
 
-        for n, gate in enumerate(GATE_ORDER[:3]):
+        def multiply(n, c, cols, sums_g, rhs, first, last):
+            sheet, plane = plane_place(n, c)
+            nc.tensor.matmul_mx(
+                out=sums_g[:, : cols.stop - cols.start],
+                lhsT=x_codes[:, c * P : (c + 1) * P].bitcast(FP8X4),
+                lhsT_scale=x_scales[:, c * P : (c + 1) * P],
+                rhs=rhs.bitcast(FP8X4),
+                rhs_scale=sheets[plane:P, sheet, cols],
+                start=first,
+                stop=last,
+            )
+
+        def load(tile_columns, source):
+            codes = stream.tile([P, LOAD_PASSES * HIDDEN], U32, align_bytes=64, tag="codes", name="codes")
+            g = source.shape[1]
+            nc.sync.dma_start(
+                out=codes[:, : g * tile_columns].rearrange("p (g n) -> p g n", g=g).bitcast(I32),
+                in_=source.bitcast(I32),
+            )
+            return codes
+
+        def words_of(gate, c0, c1):
+            if c1 <= W_PASSES:
+                return w_words[gate][c0:c1].rearrange("g p n t -> p g (n t)")
+            return u_words[gate][c0 - W_PASSES : c1 - W_PASSES].rearrange("g p n t -> p g (n t)")
+
+        for n, gate in enumerate(GATE_ORDER):
+            last_gate = gate == GATE_ORDER[-1]
             if gate == "f":
                 nc.sync.dma_start(out=old_c_rows[:], in_=old_c)
 
+            groups = [block_columns(j) for j in range(BLOCKS)]
+            if last_gate:
+                at = (BLOCKS - 1) * BANK
+                groups = groups[:-1]
+                for width in LAST_WIDTHS:
+                    groups.append(slice(at, at + width))
+                    at += width
             sums = [
-                psum.tile([P, BANK], F32, tag="bank", name="sums_%s_%d" % (gate, j))
-                for j in range(BLOCKS)
+                psum.tile([P, BANK], F32, tag="bank", name="sums_%s_%d" % (gate, g))
+                for g in range(len(groups))
             ]
-            for first_pass in range(0, PASSES, LOAD_PASSES):
-                if first_pass < W_PASSES:
-                    source = w_words[gate][first_pass : first_pass + LOAD_PASSES]
-                else:
-                    source = u_words[gate][first_pass - W_PASSES : first_pass - W_PASSES + LOAD_PASSES]
-                codes = stream.tile([P, LOAD_PASSES * HIDDEN], U32, align_bytes=64, tag="codes", name="codes")
-                nc.sync.dma_start(
-                    out=codes[:].rearrange("p (g n) -> p g n", g=LOAD_PASSES).bitcast(I32),
-                    in_=source.rearrange("g p n t -> p g (n t)").bitcast(I32),
-                )
-                for c in range(first_pass, first_pass + LOAD_PASSES):
-                    sheet, first = plane_place(n, c)
-                    for j in range(BLOCKS):
-                        at = (c - first_pass) * HIDDEN + j * BANK
-                        nc.tensor.matmul_mx(
-                            out=sums[j][:],
-                            lhsT=x_codes[:, c * P : (c + 1) * P].bitcast(FP8X4),
-                            lhsT_scale=x_scales[:, c * P : (c + 1) * P],
-                            rhs=codes[:, at : at + BANK].bitcast(FP8X4),
-                            rhs_scale=sheets[first:P, sheet, block_columns(j)],
-                            start=(c == 0),
-                            stop=(c == PASSES - 1),
-                        )
-            for j in range(BLOCKS):
-                gate_block(n, gate, j, sums[j])
+            whole_width = PASSES - O_BLOCK_PASSES if last_gate else PASSES
+            for c0 in range(0, whole_width, LOAD_PASSES):
+                c1 = min(c0 + LOAD_PASSES, whole_width)
+                codes = load(HIDDEN, words_of(gate, c0, c1))
+                for c in range(c0, c1):
+                    for g, cols in enumerate(groups):
+                        at = (c - c0) * HIDDEN + cols.start
+                        multiply(n, c, cols, sums[g], codes[:, at : at + cols.stop - cols.start], c == 0, c == PASSES - 1)
+            if not last_gate:
+                for g, cols in enumerate(groups):
+                    gate_block(n, gate, cols, sums[g])
+                continue
 
-        n = 3
-        w_by_block = w_words["o"].rearrange("g p n t -> p g (n t)")
-        u_by_block = u_words["o"].rearrange("g p n t -> p g (n t)")
-        for j in range(BLOCKS):
-            cols = block_columns(j)
-            code_bytes = slice(j * BANK * PACK, (j + 1) * BANK * PACK)
-            u_codes = stream.tile([P, LOAD_PASSES * HIDDEN], U32, align_bytes=64, tag="codes", name="u_codes")
-            nc.sync.dma_start(
-                out=u_codes[:, : U_PASSES * BANK].rearrange("p (g n) -> p g n", g=U_PASSES).bitcast(I32),
-                in_=u_by_block[:, :, code_bytes].bitcast(I32),
-            )
-            w_codes = stream.tile([P, LOAD_PASSES * HIDDEN], U32, align_bytes=64, tag="codes", name="w_codes")
-            if j < BLOCKS - 1:
-                nc.sync.dma_start(
-                    out=w_codes[:, : W_PASSES * BANK].rearrange("p (g n) -> p g n", g=W_PASSES).bitcast(I32),
-                    in_=w_by_block[:, :, code_bytes].bitcast(I32),
-                )
-            else:
-                for g in range(W_PASSES):
-                    nc.sync.dma_start(
-                        out=w_codes[:, g * BANK : (g + 1) * BANK].bitcast(I32),
-                        in_=w_by_block[:, g, code_bytes].bitcast(I32),
-                    )
-            sums_j = psum.tile([P, BANK], F32, tag="bank", name="sums_o_%d" % j)
-            order = list(range(W_PASSES, PASSES)) + list(range(W_PASSES))
-            for position, c in enumerate(order):
-                if c < W_PASSES:
-                    rhs = w_codes[:, c * BANK : (c + 1) * BANK]
+            for j in range(BLOCKS):
+                code_bytes = slice(j * BANK * PACK, (j + 1) * BANK * PACK)
+                pieces = []
+                if whole_width < W_PASSES:
+                    pieces.append((W_PASSES, PASSES))
+                    pieces.append((whole_width, W_PASSES))
                 else:
-                    rhs = u_codes[:, (c - W_PASSES) * BANK : (c - W_PASSES + 1) * BANK]
-                sheet, first = plane_place(n, c)
-                nc.tensor.matmul_mx(
-                    out=sums_j[:],
-                    lhsT=x_codes[:, c * P : (c + 1) * P].bitcast(FP8X4),
-                    lhsT_scale=x_scales[:, c * P : (c + 1) * P],
-                    rhs=rhs.bitcast(FP8X4),
-                    rhs_scale=sheets[first:P, sheet, cols],
-                    start=(position == 0),
-                    stop=(position == PASSES - 1),
-                )
-            gate_block(n, "o", j, sums_j)
+                    pieces.append((whole_width, PASSES))
+                if j == BLOCKS - 1:
+                    c0, c1 = pieces[-1]
+                    pieces = pieces[:-1] + ([(c0, c1 - 1)] if c1 - 1 > c0 else []) + [(c1 - 1, c1)]
+                order = [c for c0, c1 in pieces for c in range(c0, c1)]
+                for c0, c1 in pieces:
+                    codes = load(BANK, words_of(gate, c0, c1)[:, :, code_bytes])
+                    for c in range(c0, c1):
+                        for g, cols in enumerate(groups):
+                            if cols.start // BANK != j:
+                                continue
+                            at = (c - c0) * BANK + cols.start - j * BANK
+                            multiply(
+                                n, c, cols, sums[g], codes[:, at : at + cols.stop - cols.start],
+                                whole_width == 0 and c == order[0], c == order[-1],
+                            )
+                for g, cols in enumerate(groups):
+                    if cols.start // BANK == j:
+                        gate_block(n, gate, cols, sums[g])
 
         done = (BLOCKS - 1) * BANK
         nc.sync.dma_start(out=new_c_out, in_=new_c[:])
         nc.sync.dma_start(out=new_h_out[:, :done], in_=new_h[:, :done])
-        nc.sync.dma_start(out=new_h_out[:, done:], in_=new_h[:, done:])
+        for cols in groups[BLOCKS - 1 :]:
+            nc.sync.dma_start(out=new_h_out[:, cols], in_=new_h[:, cols])

@@ -58,7 +58,7 @@ def tile_lstmcell_w_kernel(
         stream = ctx.enter_context(tc.tile_pool(name="stream", bufs=WEIGHT_BUFFERS))
         work = ctx.enter_context(tc.tile_pool(name="work", bufs=4))
         psum = ctx.enter_context(tc.psum_pool(name="psum", bufs=8))
-        ctx.enter_context(tc.manual_schedule(engines={mybir.EngineType.SP}))
+        ctx.enter_context(tc.manual_schedule(engines={mybir.EngineType.SP, mybir.EngineType.Pool}))
 
         table_warm = keep.tile([P, 1], F32)
         nc.vector.memset(table_warm[:], 0.0)
@@ -87,21 +87,28 @@ def tile_lstmcell_w_kernel(
                 return 4 + n // 2, LIVE_ROWS * (W_PASSES * (n % 2) + c)
             return n, LIVE_ROWS * (c - W_PASSES)
 
+        def scale_load(n, gate, kind, quadrant):
+            rows = slice(LIVE_ROWS * quadrant, LIVE_ROWS * (quadrant + 1))
+            sheet, first = plane_place(n, 0 if kind == "w" else W_PASSES)
+            height = LIVE_ROWS * (W_PASSES if kind == "w" else U_PASSES)
+            start = 32 * quadrant + first
+            source = w_scales[gate] if kind == "w" else u_scales[gate]
+            nc.gpsimd.dma_start(
+                out=sheets[start : start + height, sheet, :].bitcast(F32),
+                in_=source[:, rows, :].bitcast(F32),
+            )
+
         for n, gate in enumerate(GATE_ORDER):
-            w_sheet, w_first = plane_place(n, 0)
-            u_sheet, u_first = plane_place(n, W_PASSES)
-            for quadrant in range(QUADRANTS):
-                rows = slice(LIVE_ROWS * quadrant, LIVE_ROWS * (quadrant + 1))
-                w_start = 32 * quadrant + w_first
-                nc.gpsimd.dma_start(
-                    out=sheets[w_start : w_start + W_PASSES * LIVE_ROWS, w_sheet, :].bitcast(F32),
-                    in_=w_scales[gate][:, rows, :].bitcast(F32),
-                )
-                u_start = 32 * quadrant + u_first
-                nc.gpsimd.dma_start(
-                    out=sheets[u_start : u_start + U_PASSES * LIVE_ROWS, u_sheet, :].bitcast(F32),
-                    in_=u_scales[gate][:, rows, :].bitcast(F32),
-                )
+            low, high = (0, 1), (2, 3)
+            first_half, second_half = (low, high) if n % 2 == 0 else (high, low)
+            scale_load(n, gate, "u", first_half[0])
+            scale_load(n, gate, "w", 0)
+            scale_load(n, gate, "w", 1)
+            scale_load(n, gate, "u", second_half[0])
+            scale_load(n, gate, "w", 2)
+            scale_load(n, gate, "w", 3)
+            scale_load(n, gate, "u", first_half[1])
+            scale_load(n, gate, "u", second_half[1])
 
         x_words = x_rows[:].bitcast(F32)
         grouped = keep.tile([P, PASSES, P, PACK], BF16, align_bytes=64)

@@ -158,6 +158,7 @@ def tile_lstmcell_w_kernel(
         new_h = keep.tile([P, HIDDEN], F32)
 
         O_BLOCK_PASSES = 6
+        O_LOAD_RANGES = ((0, 1024), (1024, 512), (1536, 512))
         LAST_WIDTHS = (256, 256)
 
         def gate_block(n, gate, cols, sums_g):
@@ -236,32 +237,32 @@ def tile_lstmcell_w_kernel(
                     gate_block(n, gate, cols, sums[g])
                 continue
 
-            for j in range(BLOCKS):
-                code_bytes = slice(j * BANK * PACK, (j + 1) * BANK * PACK)
+            for start, width in O_LOAD_RANGES:
+                final_range = start + width == HIDDEN
+                code_bytes = slice(start * PACK, (start + width) * PACK)
                 pieces = []
                 if whole_width < W_PASSES:
                     pieces.append((W_PASSES, PASSES))
                     pieces.append((whole_width, W_PASSES))
                 else:
                     pieces.append((whole_width, PASSES))
-                if j == BLOCKS - 1:
+                if final_range:
                     c0, c1 = pieces[-1]
                     pieces = pieces[:-1] + ([(c0, c1 - 1)] if c1 - 1 > c0 else []) + [(c1 - 1, c1)]
                 order = [c for c0, c1 in pieces for c in range(c0, c1)]
+                inside = [g for g, cols in enumerate(groups) if start <= cols.start < start + width]
                 for c0, c1 in pieces:
-                    codes = load(BANK, words_of(gate, c0, c1)[:, :, code_bytes])
+                    codes = load(width, words_of(gate, c0, c1)[:, :, code_bytes])
                     for c in range(c0, c1):
-                        for g, cols in enumerate(groups):
-                            if cols.start // BANK != j:
-                                continue
-                            at = (c - c0) * BANK + cols.start - j * BANK
+                        for g in inside:
+                            cols = groups[g]
+                            at = (c - c0) * width + cols.start - start
                             multiply(
                                 n, c, cols, sums[g], codes[:, at : at + cols.stop - cols.start],
                                 whole_width == 0 and c == order[0], c == order[-1],
                             )
-                for g, cols in enumerate(groups):
-                    if cols.start // BANK == j:
-                        gate_block(n, gate, cols, sums[g])
+                for g in inside:
+                    gate_block(n, gate, groups[g], sums[g])
 
         done = (BLOCKS - 1) * BANK
         nc.sync.dma_start(out=new_c_out, in_=new_c[:])

@@ -87,28 +87,22 @@ def tile_lstmcell_w_kernel(
                 return 4 + n // 2, LIVE_ROWS * (W_PASSES * (n % 2) + c)
             return n, LIVE_ROWS * (c - W_PASSES)
 
-        def scale_load(n, gate, kind, quadrant):
+        def scale_load(queue, dtype, n, gate, kind, quadrant):
             rows = slice(LIVE_ROWS * quadrant, LIVE_ROWS * (quadrant + 1))
             sheet, first = plane_place(n, 0 if kind == "w" else W_PASSES)
             height = LIVE_ROWS * (W_PASSES if kind == "w" else U_PASSES)
             start = 32 * quadrant + first
             source = w_scales[gate] if kind == "w" else u_scales[gate]
-            nc.gpsimd.dma_start(
-                out=sheets[start : start + height, sheet, :].bitcast(F32),
-                in_=source[:, rows, :].bitcast(F32),
+            queue.dma_start(
+                out=sheets[start : start + height, sheet, :].bitcast(dtype),
+                in_=source[:, rows, :].bitcast(dtype),
             )
 
         for n, gate in enumerate(GATE_ORDER):
-            low, high = (0, 1), (2, 3)
-            first_half, second_half = (low, high) if n % 2 == 0 else (high, low)
-            scale_load(n, gate, "u", first_half[0])
-            scale_load(n, gate, "w", 0)
-            scale_load(n, gate, "w", 1)
-            scale_load(n, gate, "u", second_half[0])
-            scale_load(n, gate, "w", 2)
-            scale_load(n, gate, "w", 3)
-            scale_load(n, gate, "u", first_half[1])
-            scale_load(n, gate, "u", second_half[1])
+            for quadrant in range(QUADRANTS):
+                scale_load(nc.gpsimd, F32, n, gate, "w", quadrant)
+            for quadrant in (2, 3):
+                scale_load(nc.gpsimd, F32, n, gate, "u", quadrant)
 
         x_words = x_rows[:].bitcast(F32)
         grouped = keep.tile([P, PASSES, P, PACK], BF16, align_bytes=64)
@@ -210,6 +204,8 @@ def tile_lstmcell_w_kernel(
 
         for n, gate in enumerate(GATE_ORDER):
             last_gate = gate == GATE_ORDER[-1]
+            for quadrant in (0, 1):
+                scale_load(nc.sync, I32, n, gate, "u", quadrant)
             if gate == "f":
                 nc.sync.dma_start(out=old_c_rows[:], in_=old_c)
 

@@ -98,11 +98,15 @@ def tile_lstmcell_w_kernel(
                 in_=source[:, rows, :].bitcast(dtype),
             )
 
-        for n, gate in enumerate(GATE_ORDER):
-            for quadrant in range(QUADRANTS):
-                scale_load(nc.gpsimd, F32, n, gate, "w", quadrant)
-            for quadrant in (2, 3):
-                scale_load(nc.gpsimd, F32, n, gate, "u", quadrant)
+        for n in range(0, len(GATE_ORDER), 2):
+            even, odd = GATE_ORDER[n], GATE_ORDER[n + 1]
+            for low_quadrant, (m, gate) in ((0, (n, even)), (1, (n + 1, odd))):
+                scale_load(nc.gpsimd, F32, n, even, "w", low_quadrant)
+                scale_load(nc.gpsimd, F32, n + 1, odd, "w", low_quadrant)
+                for quadrant in (2, 3):
+                    scale_load(nc.gpsimd, F32, m, gate, "w", quadrant)
+                for quadrant in (2, 3):
+                    scale_load(nc.gpsimd, F32, m, gate, "u", quadrant)
 
         x_words = x_rows[:].bitcast(F32)
         grouped = keep.tile([P, PASSES, P, PACK], BF16, align_bytes=64)

@@ -73,14 +73,14 @@ def tile_lstmcell_w_kernel(
         nc.sync.dma_start(out=x_rows[:, :IN_FEATURES], in_=incoming)
         nc.sync.dma_start(out=x_rows[:, IN_FEATURES:], in_=old_h)
 
+        sheets = keep.tile([P, 4 + 2, HIDDEN], U8, align_bytes=64)
+        for s in (4, 0, 5, 1, 2, 3):
+            nc.vector.memset(sheets[:, s, :].bitcast(I32), 0)
+
         bias_rows = keep.tile([P, HIDDEN], BF16)
         nc.vector.memset(bias_rows[:], 0.0)
         for n, gate in enumerate(GATE_ORDER):
             nc.scalar.dma_start(out=bias_rows[n : n + 1, :], in_=bias[gate].unsqueeze(0))
-
-        sheets = keep.tile([P, 4 + 2, HIDDEN], U8, align_bytes=64)
-        for s in range(4 + 2):
-            nc.vector.memset(sheets[:, s, :].bitcast(I32), 0)
 
         def plane_place(n, c):
             if c < W_PASSES:
@@ -206,10 +206,14 @@ def tile_lstmcell_w_kernel(
                 return w_words[gate][c0:c1].rearrange("g p n t -> p g (n t)")
             return u_words[gate][c0 - W_PASSES : c1 - W_PASSES].rearrange("g p n t -> p g (n t)")
 
-        for n, gate in enumerate(GATE_ORDER):
-            last_gate = gate == GATE_ORDER[-1]
+        def load_u_scales_low(n, gate):
             for quadrant in (0, 1):
                 scale_load(nc.sync, I32, n, gate, "u", quadrant)
+
+        for n, gate in enumerate(GATE_ORDER):
+            last_gate = gate == GATE_ORDER[-1]
+            if last_gate:
+                load_u_scales_low(n, gate)
             if gate == "f":
                 nc.sync.dma_start(out=old_c_rows[:], in_=old_c)
 
@@ -228,6 +232,8 @@ def tile_lstmcell_w_kernel(
             for c0 in range(0, whole_width, LOAD_PASSES):
                 c1 = min(c0 + LOAD_PASSES, whole_width)
                 codes = load(HIDDEN, words_of(gate, c0, c1))
+                if c0 == 0:
+                    load_u_scales_low(n, gate)
                 for c in range(c0, c1):
                     for g, cols in enumerate(groups):
                         at = (c - c0) * HIDDEN + cols.start

@@ -73,14 +73,17 @@ def tile_lstmcell_w_kernel(
         nc.sync.dma_start(out=x_rows[:, :IN_FEATURES], in_=incoming)
         nc.sync.dma_start(out=x_rows[:, IN_FEATURES:], in_=old_h)
 
+        bias_rows = keep.tile([P, BANK], BF16)
+        nc.vector.memset(bias_rows[:], 0.0)
+        for n, gate in enumerate(GATE_ORDER):
+            nc.scalar.dma_start(
+                out=bias_rows[n : n + 4 * BLOCKS - 3 : 4, :], in_=bias[gate].rearrange("(j n) -> j n", j=BLOCKS)
+            )
+
         sheets = keep.tile([P, 4 + 2, HIDDEN], U8, align_bytes=64)
         for s in (4, 0, 5, 1, 2, 3):
             nc.vector.memset(sheets[:, s, :].bitcast(I32), 0)
 
-        bias_rows = keep.tile([P, HIDDEN], BF16)
-        nc.vector.memset(bias_rows[:], 0.0)
-        for n, gate in enumerate(GATE_ORDER):
-            nc.scalar.dma_start(out=bias_rows[n : n + 1, :], in_=bias[gate].unsqueeze(0))
 
         def plane_place(n, c):
             if c < W_PASSES:
@@ -140,8 +143,8 @@ def tile_lstmcell_w_kernel(
                 spread = psum.tile([P, BANK], F32, tag="bank")
                 nc.tensor.matmul(
                     spread[:],
-                    lhsT=identity_bf16[:, n : n + 1].to_broadcast([P, P]),
-                    rhs=bias_rows[:, block_columns(j)],
+                    lhsT=identity_bf16[:, n + 4 * j : n + 4 * j + 1].to_broadcast([P, P]),
+                    rhs=bias_rows[:],
                     start=True,
                     stop=True,
                 )

@@ -248,28 +248,35 @@ def tile_lstmcell_w_kernel(
 
             for start, width in O_LOAD_RANGES:
                 final_range = start + width == HIDDEN
-                code_bytes = slice(start * PACK, (start + width) * PACK)
                 pieces = []
                 if whole_width < W_PASSES:
                     pieces.append((W_PASSES, PASSES))
                     pieces.append((whole_width, W_PASSES))
                 else:
                     pieces.append((whole_width, PASSES))
+                loads = [(c0, c1, start, width) for c0, c1 in pieces]
                 if final_range:
-                    c0, c1 = pieces[-1]
-                    pieces = pieces[:-1] + ([(c0, c1 - 1)] if c1 - 1 > c0 else []) + [(c1 - 1, c1)]
-                order = [c for c0, c1 in pieces for c in range(c0, c1)]
+                    loads = [(W_PASSES, PASSES - 1, start, width), (0, W_PASSES, start, width)]
+                    at = start
+                    for group_width in LAST_WIDTHS:
+                        loads.append((PASSES - 1, PASSES, at, group_width))
+                        at += group_width
                 inside = [g for g, cols in enumerate(groups) if start <= cols.start < start + width]
-                for c0, c1 in pieces:
-                    codes = load(width, words_of(gate, c0, c1)[:, :, code_bytes])
+                done = {g: 0 for g in inside}
+                for c0, c1, load_start, load_width in loads:
+                    code_bytes = slice(load_start * PACK, (load_start + load_width) * PACK)
+                    codes = load(load_width, words_of(gate, c0, c1)[:, :, code_bytes])
                     for c in range(c0, c1):
                         for g in inside:
                             cols = groups[g]
-                            at = (c - c0) * width + cols.start - start
+                            if not load_start <= cols.start < load_start + load_width:
+                                continue
+                            at = (c - c0) * load_width + cols.start - load_start
                             multiply(
                                 n, c, cols, sums[g], codes[:, at : at + cols.stop - cols.start],
-                                whole_width == 0 and c == order[0], c == order[-1],
+                                done[g] == 0, done[g] == PASSES - 1,
                             )
+                            done[g] += 1
                 for g in inside:
                     gate_block(n, gate, groups[g], sums[g])
 

@@ -237,8 +237,8 @@ def tile_lstmcell_w_kernel(
                 codes = load(HIDDEN, words_of(gate, c0, c1))
                 if c0 == 0:
                     load_u_scales_low(n, gate)
-                for c in range(c0, c1):
-                    for g, cols in enumerate(groups):
+                for g, cols in enumerate(groups):
+                    for c in range(c0, c1):
                         at = (c - c0) * HIDDEN + cols.start
                         multiply(n, c, cols, sums[g], codes[:, at : at + cols.stop - cols.start], c == 0, c == PASSES - 1)
             if not last_gate:
@@ -266,11 +266,11 @@ def tile_lstmcell_w_kernel(
                 for c0, c1, load_start, load_width in loads:
                     code_bytes = slice(load_start * PACK, (load_start + load_width) * PACK)
                     codes = load(load_width, words_of(gate, c0, c1)[:, :, code_bytes])
-                    for c in range(c0, c1):
-                        for g in inside:
-                            cols = groups[g]
-                            if not load_start <= cols.start < load_start + load_width:
-                                continue
+                    for g in inside:
+                        cols = groups[g]
+                        if not load_start <= cols.start < load_start + load_width:
+                            continue
+                        for c in range(c0, c1):
                             at = (c - c0) * load_width + cols.start - load_start
                             multiply(
                                 n, c, cols, sums[g], codes[:, at : at + cols.stop - cols.start],

from contextlib import ExitStack

import concourse.mybir as mybir
from concourse.masks import make_identity

F32 = mybir.dt.float32
BF16 = mybir.dt.bfloat16
I32 = mybir.dt.int32
U32 = mybir.dt.uint32
U8 = mybir.dt.uint8
FP8X4 = mybir.dt.float8_e4m3fn_x4
ACT = mybir.ActivationFunctionType

P = 128
IN_FEATURES = 1024
HIDDEN = 2048
PACK = 4
K_PASS = P * PACK
W_PASSES = IN_FEATURES // K_PASS
U_PASSES = HIDDEN // K_PASS
PASSES = W_PASSES + U_PASSES
BANK = 512
BLOCKS = HIDDEN // BANK
QUADRANTS = 4
LIVE_ROWS = 4
WORDS_PER_PASS = K_PASS // 2

GATE_ORDER = ("i", "c", "f", "o")
LOAD_PASSES = 2
WEIGHT_BUFFERS = 8

FLOPS = 2 * P * (IN_FEATURES + HIDDEN) * 4 * HIDDEN


def block_columns(j):
    return slice(j * BANK, (j + 1) * BANK)


def tile_lstmcell_w_kernel(
    tc,
    incoming, old_h, old_c,
    w_i_words, w_i_scales, b_i, u_i_words, u_i_scales,
    w_o_words, w_o_scales, b_o, u_o_words, u_o_scales,
    w_f_words, w_f_scales, b_f, u_f_words, u_f_scales,
    w_c_words, w_c_scales, b_c, u_c_words, u_c_scales,
    out_0, out_1,
):
    nc = tc.nc
    new_h_out, new_c_out = out_0, out_1
    w_words = {"i": w_i_words, "o": w_o_words, "f": w_f_words, "c": w_c_words}
    w_scales = {"i": w_i_scales, "o": w_o_scales, "f": w_f_scales, "c": w_c_scales}
    u_words = {"i": u_i_words, "o": u_o_words, "f": u_f_words, "c": u_c_words}
    u_scales = {"i": u_i_scales, "o": u_o_scales, "f": u_f_scales, "c": u_c_scales}
    bias = {"i": b_i, "o": b_o, "f": b_f, "c": b_c}

    with ExitStack() as ctx:
        keep = ctx.enter_context(tc.tile_pool(name="keep", bufs=1))
        stream = ctx.enter_context(tc.tile_pool(name="stream", bufs=WEIGHT_BUFFERS))
        work = ctx.enter_context(tc.tile_pool(name="work", bufs=4))
        psum = ctx.enter_context(tc.psum_pool(name="psum", bufs=8))
        ctx.enter_context(tc.manual_schedule(engines={mybir.EngineType.SP, mybir.EngineType.Pool}))

        table_warm = keep.tile([P, 1], F32)
        nc.vector.memset(table_warm[:], 0.0)
        nc.scalar.activation(out=table_warm[:], in_=table_warm[:], func=ACT.Sigmoid)

        identity_f32 = keep.tile([P, P], F32)
        make_identity(nc, identity_f32[:])
        identity_bf16 = keep.tile([P, P], BF16)
        make_identity(nc, identity_bf16[:])

        x_rows = keep.tile([P, IN_FEATURES + HIDDEN], BF16)
        nc.sync.dma_start(out=x_rows[:, :IN_FEATURES], in_=incoming)
        nc.sync.dma_start(out=x_rows[:, IN_FEATURES:], in_=old_h)

        bias_rows = keep.tile([P, BANK], BF16)
        nc.vector.memset(bias_rows[:], 0.0)
        for n, gate in enumerate(GATE_ORDER):
            nc.scalar.dma_start(
                out=bias_rows[n : n + 4 * BLOCKS - 3 : 4, :], in_=bias[gate].rearrange("(j n) -> j n", j=BLOCKS)
            )

        sheets = keep.tile([P, 4 + 2, HIDDEN], U8, align_bytes=64)
        for s in (4, 0, 5, 1, 2, 3):
            nc.vector.memset(sheets[:, s, :].bitcast(I32), 0)


        def plane_place(n, c):
            if c < W_PASSES:
                return 4 + n // 2, LIVE_ROWS * (W_PASSES * (n % 2) + c)
            return n, LIVE_ROWS * (c - W_PASSES)

        def scale_load(queue, dtype, n, gate, kind, quadrant):
            rows = slice(LIVE_ROWS * quadrant, LIVE_ROWS * (quadrant + 1))
            sheet, first = plane_place(n, 0 if kind == "w" else W_PASSES)
            height = LIVE_ROWS * (W_PASSES if kind == "w" else U_PASSES)
            start = 32 * quadrant + first
            source = w_scales[gate] if kind == "w" else u_scales[gate]
            queue.dma_start(
                out=sheets[start : start + height, sheet, :].bitcast(dtype),
                in_=source[:, rows, :].bitcast(dtype),
            )

        for n in range(0, len(GATE_ORDER), 2):
            even, odd = GATE_ORDER[n], GATE_ORDER[n + 1]
            for low_quadrant, (m, gate) in ((0, (n, even)), (1, (n + 1, odd))):
                scale_load(nc.gpsimd, F32, n, even, "w", low_quadrant)
                scale_load(nc.gpsimd, F32, n + 1, odd, "w", low_quadrant)
                for quadrant in (2, 3):
                    scale_load(nc.gpsimd, F32, m, gate, "w", quadrant)
                for quadrant in (2, 3):
                    scale_load(nc.gpsimd, F32, m, gate, "u", quadrant)

        x_words = x_rows[:].bitcast(F32)
        grouped = keep.tile([P, PASSES, P, PACK], BF16, align_bytes=64)
        for pair in range(PASSES // 2):
            flipped = psum.tile([P, 2, 2, P], F32, tag="bank")
            for s in range(2):
                first_word = (2 * pair + s) * WORDS_PER_PASS
                for half in range(2):
                    nc.tensor.transpose(
                        flipped[:, s, half, :],
                        x_words[:, first_word + half : first_word + WORDS_PER_PASS : 2],
                        identity_f32[:],
                    )
            nc.vector.tensor_copy(
                out=grouped[:, 2 * pair : 2 * pair + 2, :, :].bitcast(F32),
                in_=flipped[:].rearrange("p s half b -> p s b half"),
            )
        x_codes = keep.tile([P, PASSES * P], U32, align_bytes=64)
        x_scales = keep.tile([P, PASSES * P], U8, align_bytes=64)
        for pair in range(PASSES // 2):
            columns = slice(2 * pair * P, (2 * pair + 2) * P)
            nc.vector.quantize_mx(
                out=x_codes[:, columns].bitcast(FP8X4),
                scales=x_scales[:, columns],
                in_=grouped[:, 2 * pair : 2 * pair + 2, :, :].rearrange("p s b t -> p (s b t)"),
            )

        bias_all_rows = keep.tile([P, 4, HIDDEN], BF16)
        for n in range(4):
            for j in range(BLOCKS):
                spread = psum.tile([P, BANK], F32, tag="bank")
                nc.tensor.matmul(
                    spread[:],
                    lhsT=identity_bf16[:, n + 4 * j : n + 4 * j + 1].to_broadcast([P, P]),
                    rhs=bias_rows[:],
                    start=True,
                    stop=True,
                )
                if j % 2 == 0:
                    nc.scalar.copy(out=bias_all_rows[:, n, block_columns(j)], in_=spread[:])
                else:
                    nc.vector.tensor_copy(out=bias_all_rows[:, n, block_columns(j)], in_=spread[:])

        old_c_rows = keep.tile([P, HIDDEN], BF16)
        new_c = keep.tile([P, HIDDEN], F32)
        tanh_new_c = keep.tile([P, HIDDEN], F32)
        new_h = keep.tile([P, HIDDEN], F32)

        O_BLOCK_PASSES = 6
        O_LOAD_RANGES = ((0, 1024), (1024, 512), (1536, 512))
        LAST_WIDTHS = (256, 256)

        def gate_block(n, gate, cols, sums_g):
            width = cols.stop - cols.start
            with_bias = work.tile([P, BANK], F32, name="with_bias")
            nc.vector.tensor_add(out=with_bias[:, :width], in0=sums_g[:, :width], in1=bias_all_rows[:, n, cols])
            if gate == "i":
                nc.scalar.activation(out=new_c[:, cols], in_=with_bias[:, :width], func=ACT.Sigmoid)
                return
            value = work.tile([P, BANK], F32, name="value")
            nc.scalar.activation(
                out=value[:, :width], in_=with_bias[:, :width], func=ACT.Tanh if gate == "c" else ACT.Sigmoid
            )
            if gate == "c":
                nc.vector.tensor_mul(out=new_c[:, cols], in0=new_c[:, cols], in1=value[:, :width])
            if gate == "f":
                kept = work.tile([P, BANK], F32, name="kept")
                nc.vector.tensor_mul(out=kept[:, :width], in0=value[:, :width], in1=old_c_rows[:, cols])
                nc.vector.tensor_add(out=new_c[:, cols], in0=new_c[:, cols], in1=kept[:, :width])
                nc.scalar.activation(out=tanh_new_c[:, cols], in_=new_c[:, cols], func=ACT.Tanh)
            if gate == "o":
                nc.vector.tensor_mul(out=new_h[:, cols], in0=value[:, :width], in1=tanh_new_c[:, cols])

        def multiply(n, c, cols, sums_g, rhs, first, last):
            sheet, plane = plane_place(n, c)
            nc.tensor.matmul_mx(
                out=sums_g[:, : cols.stop - cols.start],
                lhsT=x_codes[:, c * P : (c + 1) * P].bitcast(FP8X4),
                lhsT_scale=x_scales[:, c * P : (c + 1) * P],
                rhs=rhs.bitcast(FP8X4),
                rhs_scale=sheets[plane:P, sheet, cols],
                start=first,
                stop=last,
            )

        def load(tile_columns, source):
            codes = stream.tile([P, LOAD_PASSES * HIDDEN], U32, align_bytes=64, tag="codes", name="codes")
            g = source.shape[1]
            nc.sync.dma_start(
                out=codes[:, : g * tile_columns].rearrange("p (g n) -> p g n", g=g).bitcast(I32),
                in_=source.bitcast(I32),
            )
            return codes

        def words_of(gate, c0, c1):
            if c1 <= W_PASSES:
                return w_words[gate][c0:c1].rearrange("g p n t -> p g (n t)")
            return u_words[gate][c0 - W_PASSES : c1 - W_PASSES].rearrange("g p n t -> p g (n t)")

        def load_u_scales_low(n, gate):
            for quadrant in (0, 1):
                scale_load(nc.sync, I32, n, gate, "u", quadrant)

        for n, gate in enumerate(GATE_ORDER):
            last_gate = gate == GATE_ORDER[-1]
            if last_gate:
                load_u_scales_low(n, gate)
            if gate == "f":
                nc.sync.dma_start(out=old_c_rows[:], in_=old_c)

            groups = [block_columns(j) for j in range(BLOCKS)]
            if last_gate:
                at = (BLOCKS - 1) * BANK
                groups = groups[:-1]
                for width in LAST_WIDTHS:
                    groups.append(slice(at, at + width))
                    at += width
            sums = [
                psum.tile([P, BANK], F32, tag="bank", name="sums_%s_%d" % (gate, g))
                for g in range(len(groups))
            ]
            whole_width = PASSES - O_BLOCK_PASSES if last_gate else PASSES
            for c0 in range(0, whole_width, LOAD_PASSES):
                c1 = min(c0 + LOAD_PASSES, whole_width)
                codes = load(HIDDEN, words_of(gate, c0, c1))
                if c0 == 0:
                    load_u_scales_low(n, gate)
                for g, cols in enumerate(groups):
                    for c in range(c0, c1):
                        at = (c - c0) * HIDDEN + cols.start
                        multiply(n, c, cols, sums[g], codes[:, at : at + cols.stop - cols.start], c == 0, c == PASSES - 1)
            if not last_gate:
                for g, cols in enumerate(groups):
                    gate_block(n, gate, cols, sums[g])
                continue

            for start, width in O_LOAD_RANGES:
                final_range = start + width == HIDDEN
                pieces = []
                if whole_width < W_PASSES:
                    pieces.append((W_PASSES, PASSES))
                    pieces.append((whole_width, W_PASSES))
                else:
                    pieces.append((whole_width, PASSES))
                loads = [(c0, c1, start, width) for c0, c1 in pieces]
                if final_range:
                    loads = [(W_PASSES, PASSES - 1, start, width), (0, W_PASSES, start, width)]
                    at = start
                    for group_width in LAST_WIDTHS:
                        loads.append((PASSES - 1, PASSES, at, group_width))
                        at += group_width
                inside = [g for g, cols in enumerate(groups) if start <= cols.start < start + width]
                done = {g: 0 for g in inside}
                for c0, c1, load_start, load_width in loads:
                    code_bytes = slice(load_start * PACK, (load_start + load_width) * PACK)
                    codes = load(load_width, words_of(gate, c0, c1)[:, :, code_bytes])
                    for g in inside:
                        cols = groups[g]
                        if not load_start <= cols.start < load_start + load_width:
                            continue
                        for c in range(c0, c1):
                            at = (c - c0) * load_width + cols.start - load_start
                            multiply(
                                n, c, cols, sums[g], codes[:, at : at + cols.stop - cols.start],
                                done[g] == 0, done[g] == PASSES - 1,
                            )
                            done[g] += 1
                for g in inside:
                    gate_block(n, gate, groups[g], sums[g])

        done = (BLOCKS - 1) * BANK
        nc.sync.dma_start(out=new_c_out, in_=new_c[:])
        nc.sync.dma_start(out=new_h_out[:, :done], in_=new_h[:, :done])
        for cols in groups[BLOCKS - 1 :]:
            nc.sync.dma_start(out=new_h_out[:, cols], in_=new_h[:, cols])
